import numpy as np
import ml_dtypes


def mxq(x, axis, fmt="e4m3"):
    dtype, down = {"e4m3": (ml_dtypes.float8_e4m3fn, 7), "e5m2": (ml_dtypes.float8_e5m2, 14)}[fmt]
    v = np.moveaxis(np.asarray(x, np.float32).astype(ml_dtypes.bfloat16).astype(np.float64), axis, -1)
    blocks = v.reshape(v.shape[:-1] + (-1, 32))
    amax = np.abs(blocks).max(-1, keepdims=True)
    byte = np.maximum(np.where(amax > 0, np.frexp(amax)[1] - 1 + 127, 0) - down, 1)
    scale = np.exp2(byte - 127.0)
    codes = (blocks / scale).astype(np.float32).astype(dtype).astype(np.float64)
    return np.moveaxis((codes * scale).reshape(v.shape), -1, axis)


WIDE = False


def mx_kscale(k):
    if not WIDE:
        return np.ones(k)
    levels = np.array([10, -10, 5, -5, 0])
    if k % 512:
        return np.exp2(np.random.permutation(np.resize(levels, k // 32))).repeat(32)
    a = np.empty((k // 512, 16))
    for p in range(k // 512):
        a[p, :8] = np.random.permutation(np.resize(levels, 8))
        for g in range(8):
            far = levels[np.abs(levels - a[p, g]) >= 10]
            a[p, g + 8] = far[np.random.randint(len(far))]
    return np.exp2(a.ravel()).repeat(32)


BF16 = ml_dtypes.bfloat16


def bf(x):
    return np.asarray(x, np.float32).astype(BF16)


def f64(x):
    return np.asarray(x).astype(np.float64)


B, L, LQ, DM, DH, W = 1, 4096, 1024, 1024, 128, 512
C = L // W


def chunk_banks(x):
    z = np.zeros_like(x[:, :1])
    prev = np.concatenate((z, x[:, :-1]), axis=1)
    nxt = np.concatenate((x[:, 1:], z), axis=1)
    return np.stack((prev, x, nxt), axis=1).sum(axis=2)


def setup_inputs():
    s = mx_kscale(DM)
    return {"kv": bf(np.random.standard_normal((B, L, DM)) * s),
            "Wkv": bf(np.random.standard_normal((DM, 2 * DH)) * 2.0 / np.sqrt(DM * C) / s[:, None])}


def reference(kv, Wkv):
    kvp = mxq(f64(kv), 2, "e4m3") @ mxq(f64(Wkv), 0, "e4m3")
    k, v = kvp[..., :DH], kvp[..., DH:]
    return chunk_banks(k.reshape(B, C, W, DH)), v

@@ -1,0 +1,227 @@
+from contextlib import ExitStack
+
+import concourse.mybir as mybir
+from concourse.masks import make_identity
+
+F32 = mybir.dt.float32
+BF16 = mybir.dt.bfloat16
+U32 = mybir.dt.uint32
+U8 = mybir.dt.uint8
+FP8X4 = mybir.dt.float8_e4m3fn_x4
+ADD = mybir.AluOpType.add
+
+P = 128
+L = 4096
+DM = 1024
+DH = 128
+CHUNK = 512
+CHUNKS = L // CHUNK
+
+FLOPS = 2 * L * DM * 2 * DH
+
+PACK = 4
+K_PASS = P * PACK
+PASSES = DM // K_PASS
+PAIRS = 2
+BLOCKS = PASSES * PAIRS
+
+ROWS = 2
+HALVES = CHUNK // (ROWS * P)
+UNITS = HALVES * CHUNKS
+UNIT_WORDS = ROWS * PASSES * P
+
+UNITS_PER_ROUND = 2
+ROUNDS = UNITS // UNITS_PER_ROUND
+ROUNDS_PER_HALF = ROUNDS // HALVES
+TRANSPOSE_BANKS = UNITS_PER_ROUND * ROWS
+
+ROUNDS_BUFFERED = 3
+
+CHUNK_ORDER = [0, CHUNKS - 1] + list(range(1, CHUNKS - 1))
+assert UNITS_PER_ROUND == 2
+
+
+def tile_localxlattention_pa_kernel(tc, kv, Wkv, out_0, out_1):
+    nc = tc.nc
+
+    kv_units = kv.rearrange(
+        "b (c h p j) k -> (b c) h p j k", c=CHUNKS, h=HALVES, p=P, j=ROWS
+    )
+    v_units = out_1.rearrange(
+        "b (c h p j) d -> (b c) h p j d", c=CHUNKS, h=HALVES, p=P, j=ROWS
+    )
+    k_ext_halves = out_0.rearrange("b s (h p j) d -> (b h) p s j d", h=HALVES, p=P, j=ROWS)
+
+    with ExitStack() as ctx:
+        ctx.enter_context(tc.manual_schedule())
+        consts = ctx.enter_context(tc.tile_pool(name="consts", bufs=1))
+        loads = ctx.enter_context(tc.tile_pool(name="loads", bufs=UNITS))
+        stage = ctx.enter_context(
+            tc.tile_pool(name="stage", bufs=ROUNDS_BUFFERED * UNITS_PER_ROUND)
+        )
+        results = ctx.enter_context(tc.tile_pool(name="results", bufs=ROUNDS))
+        xt_banks = ctx.enter_context(tc.psum_pool(name="xt_banks", bufs=TRANSPOSE_BANKS))
+        closed_banks = ctx.enter_context(tc.psum_pool(name="closed_banks", bufs=2))
+        open_banks = ctx.enter_context(tc.psum_pool(name="open_banks", bufs=ROWS))
+
+        identity = consts.tile([P, P], F32)
+        make_identity(nc, identity[:])
+
+        kv_tiles = []
+
+        def load_unit(n):
+            h, turn = divmod(n, CHUNKS)
+            x_sb = loads.tile([P, ROWS * DM], BF16)
+            nc.sync.dma_start(
+                out=x_sb[:].rearrange("p (j k) -> p j k", j=ROWS),
+                in_=kv_units[CHUNK_ORDER[turn], h],
+            )
+            kv_tiles.append(x_sb)
+
+        for n in range(UNITS_PER_ROUND):
+            load_unit(n)
+        w_raw = consts.tile([P, PASSES * PACK * 2 * DH], BF16)
+        nc.sync.dma_start(
+            out=w_raw[:].rearrange("p (g t n) -> p g t n", g=PASSES, t=PACK),
+            in_=Wkv.rearrange("(g p t) n -> p g t n", g=PASSES, p=P, t=PACK),
+        )
+        for n in range(UNITS_PER_ROUND, UNITS):
+            load_unit(n)
+
+        w_codes = consts.tile([P, PASSES * 2 * DH], U32, align_bytes=64)
+        w_scales = consts.tile([P, PASSES * 2 * DH], U8, align_bytes=64)
+
+        def quantise_weights():
+            w_grouped = consts.tile([P, PASSES * 2 * DH * PACK], BF16, align_bytes=64)
+            nc.vector.tensor_copy(
+                out=w_grouped[:].rearrange("p (g n t) -> p g n t", g=PASSES, t=PACK),
+                in_=w_raw[:].rearrange("p (g t n) -> p g n t", g=PASSES, t=PACK),
+            )
+            nc.vector.quantize_mx(
+                out=w_codes[:].bitcast(FP8X4), scales=w_scales[:], in_=w_grouped[:]
+            )
+
+        grouped_tiles = {}
+        code_tiles = {}
+
+        def transpose_round(r):
+            for i in range(UNITS_PER_ROUND):
+                n = r * UNITS_PER_ROUND + i
+                x_words = kv_tiles[n][:].bitcast(F32)
+                grouped = stage.tile([P, UNIT_WORDS * PACK], BF16, align_bytes=64)
+                grouped_words = grouped[:].bitcast(F32)
+                for j in range(ROWS):
+                    row = slice(j * BLOCKS * P, (j + 1) * BLOCKS * P)
+                    xt = xt_banks.tile([P, BLOCKS * P], F32)
+                    for s in range(BLOCKS):
+                        g, u = divmod(s, PAIRS)
+                        first = (j * PASSES + g) * PAIRS * P
+                        nc.tensor.transpose(
+                            out=xt[:, s * P : (s + 1) * P],
+                            in_=x_words[:, first + u : first + PAIRS * P : PAIRS],
+                            identity=identity[:],
+                        )
+                    copy_out = nc.vector.tensor_copy if j == 0 else nc.scalar.copy
+                    copy_out(
+                        out=grouped_words[:, row].rearrange(
+                            "p (g r u) -> p g r u", g=PASSES, u=PAIRS
+                        ),
+                        in_=xt[:].rearrange("p (g u r) -> p g r u", g=PASSES, u=PAIRS),
+                    )
+                grouped_tiles[n] = grouped
+
+        def quantise_round(r):
+            for i in range(UNITS_PER_ROUND):
+                n = r * UNITS_PER_ROUND + i
+                codes = stage.tile([P, UNIT_WORDS], U32, align_bytes=64)
+                scales = stage.tile([P, UNIT_WORDS], U8, align_bytes=64)
+                nc.vector.quantize_mx(
+                    out=codes[:].bitcast(FP8X4), scales=scales[:], in_=grouped_tiles[n][:]
+                )
+                code_tiles[n] = (codes, scales)
+
+        def multiply_row(out, n, j, w_first, opens, closes):
+            codes, scales = code_tiles[n]
+            for g in range(PASSES):
+                x_cols = slice((j * PASSES + g) * P, (j * PASSES + g + 1) * P)
+                w_cols = slice(g * 2 * DH + w_first, g * 2 * DH + w_first + DH)
+                nc.tensor.matmul_mx(
+                    out=out,
+                    lhsT=codes[:, x_cols].bitcast(FP8X4),
+                    lhsT_scale=scales[:, x_cols],
+                    rhs=w_codes[:, w_cols].bitcast(FP8X4),
+                    rhs_scale=w_scales[:, w_cols],
+                    start=(opens and g == 0),
+                    stop=(closes and g == PASSES - 1),
+                )
+
+        def multiply_closed(r, w_first):
+            products = closed_banks.tile([P, UNITS_PER_ROUND * ROWS * DH], F32)
+            for i in range(UNITS_PER_ROUND):
+                for j in range(ROWS):
+                    multiply_row(
+                        products[:, (i * ROWS + j) * DH : (i * ROWS + j + 1) * DH],
+                        r * UNITS_PER_ROUND + i, j, w_first, True, True,
+                    )
+            return products
+
+        k_ext_tiles = {}
+        middle_sums = {}
+
+        def multiply_round(r):
+            h, q = divmod(r, ROUNDS_PER_HALF)
+            half_done = q == ROUNDS_PER_HALF - 1
+            if q == 0:
+                edge_keys = multiply_closed(r, 0)
+                k_ext_sb = results.tile([P, 3 * ROWS * DH], F32)
+                k_ext_tiles[h] = k_ext_sb
+                banks = k_ext_sb[:].rearrange("p (s j d) -> p s j d", s=3, j=ROWS)
+                nc.scalar.copy(
+                    out=banks[:, 0:3:2, :, :],
+                    in_=edge_keys[:].rearrange("p (i j d) -> p i j d", i=UNITS_PER_ROUND, j=ROWS),
+                )
+                nc.vector.tensor_tensor(
+                    out=banks[:, 1, :, :], in0=banks[:, 0, :, :], in1=banks[:, 2, :, :], op=ADD
+                )
+            else:
+                if q == 1:
+                    for j in range(ROWS):
+                        middle_ps = open_banks.tile([P, DH], F32)
+                        middle_sums[(h, j)] = middle_ps
+                for i in range(UNITS_PER_ROUND):
+                    for j in range(ROWS):
+                        multiply_row(
+                            middle_sums[(h, j)][:], r * UNITS_PER_ROUND + i, j, 0,
+                            q == 1 and i == 0, half_done and i == UNITS_PER_ROUND - 1,
+                        )
+            if half_done:
+                banks = k_ext_tiles[h][:].rearrange("p (s j d) -> p s j d", s=3, j=ROWS)
+                for j in range(ROWS):
+                    nc.vector.tensor_tensor(
+                        out=banks[:, :, j, :],
+                        in0=middle_sums[(h, j)][:].unsqueeze(1).to_broadcast([P, 3, DH]),
+                        in1=banks[:, :, j, :],
+                        op=ADD,
+                    )
+
+            v_ps = multiply_closed(r, DH)
+            v_sb = results.tile([P, UNITS_PER_ROUND * ROWS * DH], F32)
+            nc.scalar.copy(out=v_sb[:], in_=v_ps[:])
+            for i in range(UNITS_PER_ROUND):
+                nc.sync.dma_start(
+                    out=v_units[CHUNK_ORDER[q * UNITS_PER_ROUND + i], h],
+                    in_=v_sb[:, i * ROWS * DH : (i + 1) * ROWS * DH].rearrange(
+                        "p (j d) -> p j d", j=ROWS
+                    ),
+                )
+            if half_done:
+                nc.sync.dma_start(out=k_ext_halves[h], in_=banks)
+
+        transpose_round(0)
+        quantise_weights()
+        quantise_round(0)
+        for r in range(1, ROUNDS):
+            transpose_round(r)
+            quantise_round(r)
+            multiply_round(r - 1)
+        multiply_round(ROUNDS - 1)

@@ -16,83 +16,76 @@ DM = 1024
 DH = 128
 CHUNK = 512
 CHUNKS = L // CHUNK
+KV = 2 * DH
 
-FLOPS = 2 * L * DM * 2 * DH
+FLOPS = 2 * L * DM * KV
 
 PACK = 4
 K_PASS = P * PACK
 PASSES = DM // K_PASS
 PAIRS = 2
-BLOCKS = PASSES * PAIRS
+ROW_WORDS = DM // 2
 
-ROWS = 2
-HALVES = CHUNK // (ROWS * P)
-UNITS = HALVES * CHUNKS
-UNIT_WORDS = ROWS * PASSES * P
+ROWS = CHUNK // P
+TWO = 2
 
-UNITS_PER_ROUND = 2
-ROUNDS = UNITS // UNITS_PER_ROUND
-ROUNDS_PER_HALF = ROUNDS // HALVES
-TRANSPOSE_BANKS = UNITS_PER_ROUND * ROWS
+CHUNK_ORDER = list(range(1, CHUNKS - 1)) + [0, CHUNKS - 1]
 
-ROUNDS_BUFFERED = 3
-
-CHUNK_ORDER = [0, CHUNKS - 1] + list(range(1, CHUNKS - 1))
-assert UNITS_PER_ROUND == 2
+FIRST_SORTED = 2
 
 
 def tile_localxlattention_pa_kernel(tc, kv, Wkv, out_0, out_1):
     nc = tc.nc
 
-    kv_units = kv.rearrange(
-        "b (c h p j) k -> (b c) h p j k", c=CHUNKS, h=HALVES, p=P, j=ROWS
-    )
-    v_units = out_1.rearrange(
-        "b (c h p j) d -> (b c) h p j d", c=CHUNKS, h=HALVES, p=P, j=ROWS
-    )
-    k_ext_halves = out_0.rearrange("b s (h p j) d -> (b h) p s j d", h=HALVES, p=P, j=ROWS)
+    kv_chunks = kv.rearrange("b (c p j) k -> (b c) p j k", c=CHUNKS, p=P, j=ROWS)
+    v_chunks = out_1.rearrange("b (c p j) d -> (b c) p j d", c=CHUNKS, p=P, j=ROWS)
+    k_ext_out = out_0.rearrange("b s (p j) d -> b p s j d", p=P, j=ROWS)[0]
 
     with ExitStack() as ctx:
         ctx.enter_context(tc.manual_schedule())
         consts = ctx.enter_context(tc.tile_pool(name="consts", bufs=1))
-        loads = ctx.enter_context(tc.tile_pool(name="loads", bufs=UNITS))
-        stage = ctx.enter_context(
-            tc.tile_pool(name="stage", bufs=ROUNDS_BUFFERED * UNITS_PER_ROUND)
-        )
-        results = ctx.enter_context(tc.tile_pool(name="results", bufs=ROUNDS))
-        xt_banks = ctx.enter_context(tc.psum_pool(name="xt_banks", bufs=TRANSPOSE_BANKS))
-        closed_banks = ctx.enter_context(tc.psum_pool(name="closed_banks", bufs=2))
-        open_banks = ctx.enter_context(tc.psum_pool(name="open_banks", bufs=ROWS))
+        loads = ctx.enter_context(tc.tile_pool(name="loads", bufs=CHUNKS))
+        sorts = ctx.enter_context(tc.tile_pool(name="sorts", bufs=2))
+        groups = ctx.enter_context(tc.tile_pool(name="groups", bufs=3))
+        results = ctx.enter_context(tc.tile_pool(name="results", bufs=CHUNKS))
+        xt_banks = ctx.enter_context(tc.psum_pool(name="xt_banks", bufs=4))
+        product_banks = ctx.enter_context(tc.psum_pool(name="product_banks", bufs=4))
 
         identity = consts.tile([P, P], F32)
         make_identity(nc, identity[:])
 
-        kv_tiles = []
-
-        def load_unit(n):
-            h, turn = divmod(n, CHUNKS)
+        x_tiles = []
+        for n in range(CHUNKS):
             x_sb = loads.tile([P, ROWS * DM], BF16)
-            nc.sync.dma_start(
-                out=x_sb[:].rearrange("p (j k) -> p j k", j=ROWS),
-                in_=kv_units[CHUNK_ORDER[turn], h],
-            )
-            kv_tiles.append(x_sb)
+            x_tiles.append(x_sb)
 
-        for n in range(UNITS_PER_ROUND):
-            load_unit(n)
-        w_raw = consts.tile([P, PASSES * PACK * 2 * DH], BF16)
+        def load_rows(n, first, count):
+            nc.sync.dma_start(
+                out=x_tiles[n][:, first * DM : (first + count) * DM].rearrange(
+                    "p (j k) -> p j k", j=count
+                ),
+                in_=kv_chunks[CHUNK_ORDER[n]][:, first : first + count, :],
+            )
+
+        for j in range(ROWS):
+            load_rows(0, j, 1)
+        load_rows(1, 0, TWO)
+        w_raw = consts.tile([P, PASSES * PACK * KV], BF16)
         nc.sync.dma_start(
             out=w_raw[:].rearrange("p (g t n) -> p g t n", g=PASSES, t=PACK),
             in_=Wkv.rearrange("(g p t) n -> p g t n", g=PASSES, p=P, t=PACK),
         )
-        for n in range(UNITS_PER_ROUND, UNITS):
-            load_unit(n)
+        load_rows(1, TWO, TWO)
+        for n in range(2, CHUNKS - 1):
+            load_rows(n, 0, ROWS)
+        for j in range(0, ROWS, TWO):
+            load_rows(CHUNKS - 1, j, TWO)
 
-        w_codes = consts.tile([P, PASSES * 2 * DH], U32, align_bytes=64)
-        w_scales = consts.tile([P, PASSES * 2 * DH], U8, align_bytes=64)
+        w_codes = consts.tile([P, PASSES * KV], U32, align_bytes=64)
+        w_scales = consts.tile([P, PASSES * KV], U8, align_bytes=64)
 
         def quantise_weights():
-            w_grouped = consts.tile([P, PASSES * 2 * DH * PACK], BF16, align_bytes=64)
+            w_grouped = consts.tile([P, PASSES * KV * PACK], BF16, align_bytes=64)
             nc.vector.tensor_copy(
                 out=w_grouped[:].rearrange("p (g n t) -> p g n t", g=PASSES, t=PACK),
                 in_=w_raw[:].rearrange("p (g t n) -> p g n t", g=PASSES, t=PACK),
@@ -101,127 +94,120 @@ def tile_localxlattention_pa_kernel(tc, kv, Wkv, out_0, out_1):
                 out=w_codes[:].bitcast(FP8X4), scales=w_scales[:], in_=w_grouped[:]
             )
 
+        sorted_tiles = {}
         grouped_tiles = {}
         code_tiles = {}
 
-        def transpose_round(r):
-            for i in range(UNITS_PER_ROUND):
-                n = r * UNITS_PER_ROUND + i
-                x_words = kv_tiles[n][:].bitcast(F32)
-                grouped = stage.tile([P, UNIT_WORDS * PACK], BF16, align_bytes=64)
-                grouped_words = grouped[:].bitcast(F32)
-                for j in range(ROWS):
-                    row = slice(j * BLOCKS * P, (j + 1) * BLOCKS * P)
-                    xt = xt_banks.tile([P, BLOCKS * P], F32)
-                    for s in range(BLOCKS):
-                        g, u = divmod(s, PAIRS)
-                        first = (j * PASSES + g) * PAIRS * P
+        def sort_chunk(n):
+            sorted_sb = sorts.tile([P, ROWS * ROW_WORDS], F32)
+            nc.vector.tensor_copy(
+                out=sorted_sb[:].rearrange("p (g u w) -> p g u w", g=ROWS * PASSES, u=PAIRS),
+                in_=x_tiles[n][:].bitcast(F32).rearrange(
+                    "p (g w u) -> p g u w", g=ROWS * PASSES, u=PAIRS
+                ),
+            )
+            sorted_tiles[n] = sorted_sb
+
+        def transpose_chunk(n):
+            x_words = x_tiles[n][:].bitcast(F32)
+            grouped = groups.tile([P, ROWS * DM], BF16, align_bytes=64)
+            grouped_tiles[n] = grouped
+            for j in range(ROWS):
+                xt = xt_banks.tile([P, ROW_WORDS], F32)
+                for g in range(PASSES):
+                    for u in range(PAIRS):
+                        s = g * PAIRS + u
+                        first = j * ROW_WORDS + g * PAIRS * P
+                        if n in sorted_tiles:
+                            first += u * P
+                            words = sorted_tiles[n][:, first : first + P]
+                        else:
+                            words = x_words[:, first + u : first + PAIRS * P : PAIRS]
                         nc.tensor.transpose(
-                            out=xt[:, s * P : (s + 1) * P],
-                            in_=x_words[:, first + u : first + PAIRS * P : PAIRS],
-                            identity=identity[:],
+                            out=xt[:, s * P : (s + 1) * P], in_=words, identity=identity[:]
                         )
-                    copy_out = nc.vector.tensor_copy if j == 0 else nc.scalar.copy
-                    copy_out(
-                        out=grouped_words[:, row].rearrange(
-                            "p (g r u) -> p g r u", g=PASSES, u=PAIRS
-                        ),
-                        in_=xt[:].rearrange("p (g u r) -> p g r u", g=PASSES, u=PAIRS),
-                    )
-                grouped_tiles[n] = grouped
+                on_vector = j % TWO == 0 and n in (0, CHUNKS - 1)
+                copy_out = nc.vector.tensor_copy if on_vector else nc.scalar.copy
+                copy_out(
+                    out=grouped[:].bitcast(F32)[:, j * ROW_WORDS : (j + 1) * ROW_WORDS].rearrange(
+                        "p (g r u) -> p g r u", g=PASSES, u=PAIRS
+                    ),
+                    in_=xt[:].rearrange("p (g u r) -> p g r u", g=PASSES, u=PAIRS),
+                )
 
-        def quantise_round(r):
-            for i in range(UNITS_PER_ROUND):
-                n = r * UNITS_PER_ROUND + i
-                codes = stage.tile([P, UNIT_WORDS], U32, align_bytes=64)
-                scales = stage.tile([P, UNIT_WORDS], U8, align_bytes=64)
+        def quantise_chunk(n, pieces):
+            codes = groups.tile([P, ROWS * PASSES * P], U32, align_bytes=64)
+            scales = groups.tile([P, ROWS * PASSES * P], U8, align_bytes=64)
+            width = ROWS * PASSES * P // pieces
+            for i in range(pieces):
+                words = slice(i * width, (i + 1) * width)
                 nc.vector.quantize_mx(
-                    out=codes[:].bitcast(FP8X4), scales=scales[:], in_=grouped_tiles[n][:]
+                    out=codes[:, words].bitcast(FP8X4),
+                    scales=scales[:, words],
+                    in_=grouped_tiles[n][:, i * width * PACK : (i + 1) * width * PACK],
                 )
-                code_tiles[n] = (codes, scales)
+            code_tiles[n] = (codes, scales)
 
-        def multiply_row(out, n, j, w_first, opens, closes):
+        def multiply_rows(n, w_first):
             codes, scales = code_tiles[n]
-            for g in range(PASSES):
-                x_cols = slice((j * PASSES + g) * P, (j * PASSES + g + 1) * P)
-                w_cols = slice(g * 2 * DH + w_first, g * 2 * DH + w_first + DH)
-                nc.tensor.matmul_mx(
-                    out=out,
-                    lhsT=codes[:, x_cols].bitcast(FP8X4),
-                    lhsT_scale=scales[:, x_cols],
-                    rhs=w_codes[:, w_cols].bitcast(FP8X4),
-                    rhs_scale=w_scales[:, w_cols],
-                    start=(opens and g == 0),
-                    stop=(closes and g == PASSES - 1),
-                )
-
-        def multiply_closed(r, w_first):
-            products = closed_banks.tile([P, UNITS_PER_ROUND * ROWS * DH], F32)
-            for i in range(UNITS_PER_ROUND):
-                for j in range(ROWS):
-                    multiply_row(
-                        products[:, (i * ROWS + j) * DH : (i * ROWS + j + 1) * DH],
-                        r * UNITS_PER_ROUND + i, j, w_first, True, True,
+            products = product_banks.tile([P, ROWS * DH], F32)
+            for j in range(ROWS):
+                for g in range(PASSES):
+                    x_cols = slice((j * PASSES + g) * P, (j * PASSES + g + 1) * P)
+                    w_cols = slice(g * KV + w_first, g * KV + w_first + DH)
+                    nc.tensor.matmul_mx(
+                        out=products[:, j * DH : (j + 1) * DH],
+                        lhsT=codes[:, x_cols].bitcast(FP8X4),
+                        lhsT_scale=scales[:, x_cols],
+                        rhs=w_codes[:, w_cols].bitcast(FP8X4),
+                        rhs_scale=w_scales[:, w_cols],
+                        start=(g == 0),
+                        stop=(g == PASSES - 1),
                     )
             return products
 
-        k_ext_tiles = {}
-        middle_sums = {}
+        k_ext_sb = consts.tile([P, 3 * ROWS * DH], F32)
+        sum_0, sum_1, sum_2 = (
+            k_ext_sb[:, s * ROWS * DH : (s + 1) * ROWS * DH] for s in range(3)
+        )
+        banks = k_ext_sb[:].rearrange("p (s j d) -> p s j d", s=3, j=ROWS)
 
-        def multiply_round(r):
-            h, q = divmod(r, ROUNDS_PER_HALF)
-            half_done = q == ROUNDS_PER_HALF - 1
-            if q == 0:
-                edge_keys = multiply_closed(r, 0)
-                k_ext_sb = results.tile([P, 3 * ROWS * DH], F32)
-                k_ext_tiles[h] = k_ext_sb
-                banks = k_ext_sb[:].rearrange("p (s j d) -> p s j d", s=3, j=ROWS)
-                nc.scalar.copy(
-                    out=banks[:, 0:3:2, :, :],
-                    in_=edge_keys[:].rearrange("p (i j d) -> p i j d", i=UNITS_PER_ROUND, j=ROWS),
-                )
-                nc.vector.tensor_tensor(
-                    out=banks[:, 1, :, :], in0=banks[:, 0, :, :], in1=banks[:, 2, :, :], op=ADD
-                )
+        def multiply_chunk(n):
+            c = CHUNK_ORDER[n]
+            keys = multiply_rows(n, 0)
+            if n == 0:
+                nc.scalar.copy(out=sum_2, in_=keys[:])
+            elif c == 0:
+                nc.vector.tensor_tensor(out=sum_0, in0=keys[:], in1=sum_2, op=ADD)
+                nc.sync.dma_start(out=k_ext_out[:, 0, :, :], in_=banks[:, 0, :, :])
             else:
-                if q == 1:
-                    for j in range(ROWS):
-                        middle_ps = open_banks.tile([P, DH], F32)
-                        middle_sums[(h, j)] = middle_ps
-                for i in range(UNITS_PER_ROUND):
-                    for j in range(ROWS):
-                        multiply_row(
-                            middle_sums[(h, j)][:], r * UNITS_PER_ROUND + i, j, 0,
-                            q == 1 and i == 0, half_done and i == UNITS_PER_ROUND - 1,
-                        )
-            if half_done:
-                banks = k_ext_tiles[h][:].rearrange("p (s j d) -> p s j d", s=3, j=ROWS)
-                for j in range(ROWS):
-                    nc.vector.tensor_tensor(
-                        out=banks[:, :, j, :],
-                        in0=middle_sums[(h, j)][:].unsqueeze(1).to_broadcast([P, 3, DH]),
-                        in1=banks[:, :, j, :],
-                        op=ADD,
-                    )
+                if c == CHUNKS - 1:
+                    nc.vector.tensor_tensor(out=sum_1, in0=keys[:], in1=sum_0, op=ADD)
+                nc.vector.tensor_tensor(out=sum_2, in0=keys[:], in1=sum_2, op=ADD)
+            values = multiply_rows(n, DH)
+            v_sb = results.tile([P, ROWS * DH], F32)
+            nc.scalar.copy(out=v_sb[:], in_=values[:])
+            if c == CHUNKS - 1:
+                nc.sync.dma_start(out=k_ext_out[:, 1:3, :, :], in_=banks[:, 1:3, :, :])
+            nc.sync.dma_start(
+                out=v_chunks[c], in_=v_sb[:].rearrange("p (j d) -> p j d", j=ROWS)
+            )
 
-            v_ps = multiply_closed(r, DH)
-            v_sb = results.tile([P, UNITS_PER_ROUND * ROWS * DH], F32)
-            nc.scalar.copy(out=v_sb[:], in_=v_ps[:])
-            for i in range(UNITS_PER_ROUND):
-                nc.sync.dma_start(
-                    out=v_units[CHUNK_ORDER[q * UNITS_PER_ROUND + i], h],
-                    in_=v_sb[:, i * ROWS * DH : (i + 1) * ROWS * DH].rearrange(
-                        "p (j d) -> p j d", j=ROWS
-                    ),
-                )
-            if half_done:
-                nc.sync.dma_start(out=k_ext_halves[h], in_=banks)
-
-        transpose_round(0)
-        quantise_weights()
-        quantise_round(0)
-        for r in range(1, ROUNDS):
-            transpose_round(r)
-            quantise_round(r)
-            multiply_round(r - 1)
-        multiply_round(ROUNDS - 1)
+        for n in range(CHUNKS):
+            if n == 1:
+                quantise_weights()
+                quantise_chunk(0, 2)
+            if FIRST_SORTED <= n + 1 < CHUNKS - 1:
+                sort_chunk(n + 1)
+            if n >= 2:
+                quantise_chunk(n - 1, 1)
+            if n == CHUNKS - 1:
+                multiply_chunk(n - 2)
+            transpose_chunk(n)
+            if n == 1:
+                multiply_chunk(0)
+            if 3 <= n < CHUNKS - 1:
+                multiply_chunk(n - 2)
+        quantise_chunk(CHUNKS - 1, 2)
+        multiply_chunk(CHUNKS - 2)
+        multiply_chunk(CHUNKS - 1)

@@ -31,7 +31,7 @@ TWO = 2
 
 CHUNK_ORDER = list(range(1, CHUNKS - 1)) + [0, CHUNKS - 1]
 
-FIRST_SORTED = 2
+MIDDLE = CHUNKS - 2
 
 
 def tile_localxlattention_pa_kernel(tc, kv, Wkv, out_0, out_1):
@@ -47,6 +47,7 @@ def tile_localxlattention_pa_kernel(tc, kv, Wkv, out_0, out_1):
         loads = ctx.enter_context(tc.tile_pool(name="loads", bufs=CHUNKS))
         sorts = ctx.enter_context(tc.tile_pool(name="sorts", bufs=2))
         groups = ctx.enter_context(tc.tile_pool(name="groups", bufs=3))
+        codes_pool = ctx.enter_context(tc.tile_pool(name="codes_pool", bufs=4))
         results = ctx.enter_context(tc.tile_pool(name="results", bufs=CHUNKS))
         xt_banks = ctx.enter_context(tc.psum_pool(name="xt_banks", bufs=4))
         product_banks = ctx.enter_context(tc.psum_pool(name="product_banks", bufs=4))
@@ -67,49 +68,54 @@ def tile_localxlattention_pa_kernel(tc, kv, Wkv, out_0, out_1):
                 in_=kv_chunks[CHUNK_ORDER[n]][:, first : first + count, :],
             )
 
-        for j in range(ROWS):
-            load_rows(0, j, 1)
-        load_rows(1, 0, TWO)
         w_raw = consts.tile([P, PASSES * PACK * KV], BF16)
-        nc.sync.dma_start(
-            out=w_raw[:].rearrange("p (g t n) -> p g t n", g=PASSES, t=PACK),
-            in_=Wkv.rearrange("(g p t) n -> p g t n", g=PASSES, p=P, t=PACK),
+        w_rows = Wkv.rearrange(
+            "(g r u w e) n -> g w r u (e n)", g=PASSES, r=P // 2, u=PAIRS, w=2, e=2
         )
-        load_rows(1, TWO, TWO)
-        for n in range(2, CHUNKS - 1):
-            load_rows(n, 0, ROWS)
-        for j in range(0, ROWS, TWO):
-            load_rows(CHUNKS - 1, j, TWO)
+        for g in range(PASSES):
+            for w in range(2):
+                nc.sync.dma_start(
+                    out=w_raw[w:P:2, g * PACK * KV : (g + 1) * PACK * KV].rearrange(
+                        "r (u c) -> r u c", u=PAIRS
+                    ),
+                    in_=w_rows[g, w],
+                )
+        for n in range(CHUNKS):
+            count = 1 if n == 0 else TWO
+            for j in range(0, ROWS, count):
+                load_rows(n, j, count)
 
         w_codes = consts.tile([P, PASSES * KV], U32, align_bytes=64)
         w_scales = consts.tile([P, PASSES * KV], U8, align_bytes=64)
 
-        def quantise_weights():
-            w_grouped = consts.tile([P, PASSES * KV * PACK], BF16, align_bytes=64)
+        w_grouped = consts.tile([P, PASSES * KV * PACK], BF16, align_bytes=64)
+
+        def group_weights(g):
+            values = slice(g * KV * PACK, (g + 1) * KV * PACK)
             nc.vector.tensor_copy(
-                out=w_grouped[:].rearrange("p (g n t) -> p g n t", g=PASSES, t=PACK),
-                in_=w_raw[:].rearrange("p (g t n) -> p g n t", g=PASSES, t=PACK),
-            )
-            nc.vector.quantize_mx(
-                out=w_codes[:].bitcast(FP8X4), scales=w_scales[:], in_=w_grouped[:]
+                out=w_grouped[:, values].rearrange("p (n t) -> p n t", t=PACK),
+                in_=w_raw[:, values].rearrange("p (t n) -> p n t", t=PACK),
             )
 
         sorted_tiles = {}
         grouped_tiles = {}
         code_tiles = {}
 
-        def sort_chunk(n):
-            sorted_sb = sorts.tile([P, ROWS * ROW_WORDS], F32)
+        def sort_rows(n, j, count):
+            if j == 0:
+                sorted_sb = sorts.tile([P, ROWS * ROW_WORDS], F32)
+                sorted_tiles[n] = sorted_sb
+            words = slice(j * ROW_WORDS, (j + count) * ROW_WORDS)
             nc.vector.tensor_copy(
-                out=sorted_sb[:].rearrange("p (g u w) -> p g u w", g=ROWS * PASSES, u=PAIRS),
-                in_=x_tiles[n][:].bitcast(F32).rearrange(
-                    "p (g w u) -> p g u w", g=ROWS * PASSES, u=PAIRS
+                out=sorted_tiles[n][:, words].rearrange(
+                    "p (g u c) -> p g u c", g=count * PASSES, u=PAIRS
+                ),
+                in_=x_tiles[n][:].bitcast(F32)[:, words].rearrange(
+                    "p (g r u w) -> p g u r w", g=count * PASSES, u=PAIRS, w=2
                 ),
             )
-            sorted_tiles[n] = sorted_sb
 
         def transpose_chunk(n):
-            x_words = x_tiles[n][:].bitcast(F32)
             grouped = groups.tile([P, ROWS * DM], BF16, align_bytes=64)
             grouped_tiles[n] = grouped
             for j in range(ROWS):
@@ -117,16 +123,13 @@ def tile_localxlattention_pa_kernel(tc, kv, Wkv, out_0, out_1):
                 for g in range(PASSES):
                     for u in range(PAIRS):
                         s = g * PAIRS + u
-                        first = j * ROW_WORDS + g * PAIRS * P
-                        if n in sorted_tiles:
-                            first += u * P
-                            words = sorted_tiles[n][:, first : first + P]
-                        else:
-                            words = x_words[:, first + u : first + PAIRS * P : PAIRS]
+                        first = j * ROW_WORDS + s * P
                         nc.tensor.transpose(
-                            out=xt[:, s * P : (s + 1) * P], in_=words, identity=identity[:]
+                            out=xt[:, s * P : (s + 1) * P],
+                            in_=sorted_tiles[n][:, first : first + P],
+                            identity=identity[:],
                         )
-                on_vector = j % TWO == 0 and n in (0, CHUNKS - 1)
+                on_vector = j % TWO == 0 and n == CHUNKS - 1
                 copy_out = nc.vector.tensor_copy if on_vector else nc.scalar.copy
                 copy_out(
                     out=grouped[:].bitcast(F32)[:, j * ROW_WORDS : (j + 1) * ROW_WORDS].rearrange(
@@ -135,79 +138,119 @@ def tile_localxlattention_pa_kernel(tc, kv, Wkv, out_0, out_1):
                     in_=xt[:].rearrange("p (g u r) -> p g r u", g=PASSES, u=PAIRS),
                 )
 
-        def quantise_chunk(n, pieces):
-            codes = groups.tile([P, ROWS * PASSES * P], U32, align_bytes=64)
-            scales = groups.tile([P, ROWS * PASSES * P], U8, align_bytes=64)
-            width = ROWS * PASSES * P // pieces
-            for i in range(pieces):
-                words = slice(i * width, (i + 1) * width)
-                nc.vector.quantize_mx(
-                    out=codes[:, words].bitcast(FP8X4),
-                    scales=scales[:, words],
-                    in_=grouped_tiles[n][:, i * width * PACK : (i + 1) * width * PACK],
-                )
-            code_tiles[n] = (codes, scales)
-
-        def multiply_rows(n, w_first):
+        def quantise_rows(n, j, count):
+            if j == 0:
+                codes = codes_pool.tile([P, ROWS * PASSES * P], U32, align_bytes=64)
+                scales = codes_pool.tile([P, ROWS * PASSES * P], U8, align_bytes=64)
+                code_tiles[n] = (codes, scales)
             codes, scales = code_tiles[n]
+            words = slice(j * PASSES * P, (j + count) * PASSES * P)
+            nc.vector.quantize_mx(
+                out=codes[:, words].bitcast(FP8X4),
+                scales=scales[:, words],
+                in_=grouped_tiles[n][:, j * DM : (j + count) * DM],
+            )
+
+        def multiply_rows(chunks, rows, w_first):
             products = product_banks.tile([P, ROWS * DH], F32)
-            for j in range(ROWS):
-                for g in range(PASSES):
+            for i, j in enumerate(rows):
+                passes = [(n, g) for n in chunks for g in range(PASSES)]
+                for n, g in passes:
+                    codes, scales = code_tiles[n]
                     x_cols = slice((j * PASSES + g) * P, (j * PASSES + g + 1) * P)
                     w_cols = slice(g * KV + w_first, g * KV + w_first + DH)
                     nc.tensor.matmul_mx(
-                        out=products[:, j * DH : (j + 1) * DH],
+                        out=products[:, i * DH : (i + 1) * DH],
                         lhsT=codes[:, x_cols].bitcast(FP8X4),
                         lhsT_scale=scales[:, x_cols],
                         rhs=w_codes[:, w_cols].bitcast(FP8X4),
                         rhs_scale=w_scales[:, w_cols],
-                        start=(g == 0),
-                        stop=(g == PASSES - 1),
+                        start=((n, g) == passes[0]),
+                        stop=((n, g) == passes[-1]),
                     )
             return products
 
         k_ext_sb = consts.tile([P, 3 * ROWS * DH], F32)
-        sum_0, sum_1, sum_2 = (
-            k_ext_sb[:, s * ROWS * DH : (s + 1) * ROWS * DH] for s in range(3)
-        )
-        banks = k_ext_sb[:].rearrange("p (s j d) -> p s j d", s=3, j=ROWS)
+        banks = k_ext_sb[:].rearrange("p (s c) -> p s c", s=3)
+        bank_rows = k_ext_sb[:].rearrange("p (s j d) -> p s j d", s=3, j=ROWS)
+        all_rows = range(ROWS)
 
-        def multiply_chunk(n):
-            c = CHUNK_ORDER[n]
-            keys = multiply_rows(n, 0)
-            if n == 0:
-                nc.scalar.copy(out=sum_2, in_=keys[:])
-            elif c == 0:
-                nc.vector.tensor_tensor(out=sum_0, in0=keys[:], in1=sum_2, op=ADD)
-                nc.sync.dma_start(out=k_ext_out[:, 0, :, :], in_=banks[:, 0, :, :])
-            else:
-                if c == CHUNKS - 1:
-                    nc.vector.tensor_tensor(out=sum_1, in0=keys[:], in1=sum_0, op=ADD)
-                nc.vector.tensor_tensor(out=sum_2, in0=keys[:], in1=sum_2, op=ADD)
-            values = multiply_rows(n, DH)
+        def multiply_values(n):
+            values = multiply_rows([n], all_rows, DH)
             v_sb = results.tile([P, ROWS * DH], F32)
             nc.scalar.copy(out=v_sb[:], in_=values[:])
-            if c == CHUNKS - 1:
-                nc.sync.dma_start(out=k_ext_out[:, 1:3, :, :], in_=banks[:, 1:3, :, :])
             nc.sync.dma_start(
-                out=v_chunks[c], in_=v_sb[:].rearrange("p (j d) -> p j d", j=ROWS)
+                out=v_chunks[CHUNK_ORDER[n]], in_=v_sb[:].rearrange("p (j d) -> p j d", j=ROWS)
             )
 
+        def multiply_chunk(n):
+            if n == MIDDLE:
+                keys = multiply_rows([n], all_rows, 0)
+                nc.vector.tensor_tensor(out=banks[:, 0, :], in0=keys[:], in1=banks[:, 2, :], op=ADD)
+                nc.sync.dma_start(
+                    out=k_ext_out[:, 0, :, :], in_=bank_rows[:, 0, :, :]
+                )
+            elif n % TWO == 1:
+                keys = multiply_rows([n - 1, n], all_rows, 0)
+                if n == 1:
+                    nc.scalar.copy(out=banks[:, 2, :], in_=keys[:])
+                else:
+                    nc.vector.tensor_tensor(
+                        out=banks[:, 2, :], in0=keys[:], in1=banks[:, 2, :], op=ADD
+                    )
+            multiply_values(n)
+
+        def multiply_last_chunk(n):
+            v_sb = results.tile([P, ROWS * DH], F32)
+            v_rows = v_sb[:].rearrange("p (j d) -> p j d", j=ROWS)
+            for j in range(0, ROWS, TWO):
+                rows = slice(j, j + TWO)
+                cols = slice(j * DH, (j + TWO) * DH)
+                keys = multiply_rows([n], range(j, j + TWO), 0)[:, 0 : TWO * DH]
+                for s, before in ((1, 0), (2, 2)):
+                    nc.vector.tensor_tensor(
+                        out=banks[:, s, cols], in0=keys, in1=banks[:, before, cols], op=ADD
+                    )
+                values = multiply_rows([n], range(j, j + TWO), DH)[:, 0 : TWO * DH]
+                nc.scalar.copy(out=v_sb[:, cols], in_=values)
+                nc.sync.dma_start(
+                    out=v_chunks[CHUNK_ORDER[n]][:, rows, :], in_=v_rows[:, rows, :]
+                )
+                nc.sync.dma_start(
+                    out=k_ext_out[:, 1:3, rows, :], in_=bank_rows[:, 1:3, rows, :]
+                )
+
+        last = CHUNKS - 1
+        group_weights(0)
+        sort_rows(0, 0, 1)
+        group_weights(1)
+        for j in range(1, ROWS):
+            sort_rows(0, j, 1)
+        nc.vector.quantize_mx(
+            out=w_codes[:].bitcast(FP8X4), scales=w_scales[:], in_=w_grouped[:]
+        )
+        sort_rows(1, 0, TWO)
         for n in range(CHUNKS):
             if n == 1:
-                quantise_weights()
-                quantise_chunk(0, 2)
-            if FIRST_SORTED <= n + 1 < CHUNKS - 1:
-                sort_chunk(n + 1)
-            if n >= 2:
-                quantise_chunk(n - 1, 1)
-            if n == CHUNKS - 1:
+                quantise_rows(0, 0, TWO)
+                sort_rows(1, TWO, TWO)
+                quantise_rows(0, TWO, TWO)
+                sort_rows(2, 0, TWO)
+                sort_rows(2, TWO, TWO)
+            elif n > 1:
+                for j in range(0, ROWS, TWO):
+                    quantise_rows(n - 1, j, TWO)
+                    if n < last:
+                        sort_rows(n + 1, j, TWO)
+            if n == last:
                 multiply_chunk(n - 2)
             transpose_chunk(n)
             if n == 1:
                 multiply_chunk(0)
-            if 3 <= n < CHUNKS - 1:
+            if 3 <= n < last:
                 multiply_chunk(n - 2)
-        quantise_chunk(CHUNKS - 1, 2)
-        multiply_chunk(CHUNKS - 2)
-        multiply_chunk(CHUNKS - 1)
+        quantise_rows(last, 0, TWO)
+        for j in range(TWO, ROWS):
+            quantise_rows(last, j, 1)
+        multiply_chunk(last - 1)
+        multiply_last_chunk(last)

@@ -80,8 +80,9 @@ def tile_localxlattention_pa_kernel(tc, kv, Wkv, out_0, out_1):
                     ),
                     in_=w_rows[g, w],
                 )
+        rows_at_once = {0: 1, 1: TWO, 2: TWO, 3: TWO, CHUNKS - 1: TWO}
         for n in range(CHUNKS):
-            count = 1 if n == 0 else TWO
+            count = rows_at_once.get(n, ROWS)
             for j in range(0, ROWS, count):
                 load_rows(n, j, count)
 
@@ -129,7 +130,7 @@ def tile_localxlattention_pa_kernel(tc, kv, Wkv, out_0, out_1):
                             in_=sorted_tiles[n][:, first : first + P],
                             identity=identity[:],
                         )
-                on_vector = j % TWO == 0 and n == CHUNKS - 1
+                on_vector = j == 0 and n == CHUNKS - 1
                 copy_out = nc.vector.tensor_copy if on_vector else nc.scalar.copy
                 copy_out(
                     out=grouped[:].bitcast(F32)[:, j * ROW_WORDS : (j + 1) * ROW_WORDS].rearrange(
@@ -151,8 +152,7 @@ def tile_localxlattention_pa_kernel(tc, kv, Wkv, out_0, out_1):
                 in_=grouped_tiles[n][:, j * DM : (j + count) * DM],
             )
 
-        def multiply_rows(chunks, rows, w_first):
-            products = product_banks.tile([P, ROWS * DH], F32)
+        def multiply_rows(products, chunks, rows, w_first):
             for i, j in enumerate(rows):
                 passes = [(n, g) for n in chunks for g in range(PASSES)]
                 for n, g in passes:
@@ -168,7 +168,6 @@ def tile_localxlattention_pa_kernel(tc, kv, Wkv, out_0, out_1):
                         start=((n, g) == passes[0]),
                         stop=((n, g) == passes[-1]),
                     )
-            return products
 
         k_ext_sb = consts.tile([P, 3 * ROWS * DH], F32)
         banks = k_ext_sb[:].rearrange("p (s c) -> p s c", s=3)
@@ -176,27 +175,32 @@ def tile_localxlattention_pa_kernel(tc, kv, Wkv, out_0, out_1):
         all_rows = range(ROWS)
 
         def multiply_values(n):
-            values = multiply_rows([n], all_rows, DH)
+            products = product_banks.tile([P, ROWS * DH], F32)
+            multiply_rows(products, [n], all_rows, DH)
             v_sb = results.tile([P, ROWS * DH], F32)
-            nc.scalar.copy(out=v_sb[:], in_=values[:])
+            nc.scalar.copy(out=v_sb[:], in_=products[:])
             nc.sync.dma_start(
                 out=v_chunks[CHUNK_ORDER[n]], in_=v_sb[:].rearrange("p (j d) -> p j d", j=ROWS)
             )
 
         def multiply_chunk(n):
             if n == MIDDLE:
-                keys = multiply_rows([n], all_rows, 0)
-                nc.vector.tensor_tensor(out=banks[:, 0, :], in0=keys[:], in1=banks[:, 2, :], op=ADD)
+                products = product_banks.tile([P, ROWS * DH], F32)
+                multiply_rows(products, [n], all_rows, 0)
+                nc.vector.tensor_tensor(
+                    out=banks[:, 0, :], in0=products[:], in1=banks[:, 2, :], op=ADD
+                )
                 nc.sync.dma_start(
                     out=k_ext_out[:, 0, :, :], in_=bank_rows[:, 0, :, :]
                 )
             elif n % TWO == 1:
-                keys = multiply_rows([n - 1, n], all_rows, 0)
+                products = product_banks.tile([P, ROWS * DH], F32)
+                multiply_rows(products, [n - 1, n], all_rows, 0)
                 if n == 1:
-                    nc.scalar.copy(out=banks[:, 2, :], in_=keys[:])
+                    nc.scalar.copy(out=banks[:, 2, :], in_=products[:])
                 else:
                     nc.vector.tensor_tensor(
-                        out=banks[:, 2, :], in0=keys[:], in1=banks[:, 2, :], op=ADD
+                        out=banks[:, 2, :], in0=products[:], in1=banks[:, 2, :], op=ADD
                     )
             multiply_values(n)
 
@@ -206,13 +210,17 @@ def tile_localxlattention_pa_kernel(tc, kv, Wkv, out_0, out_1):
             for j in range(0, ROWS, TWO):
                 rows = slice(j, j + TWO)
                 cols = slice(j * DH, (j + TWO) * DH)
-                keys = multiply_rows([n], range(j, j + TWO), 0)[:, 0 : TWO * DH]
-                for s, before in ((1, 0), (2, 2)):
-                    nc.vector.tensor_tensor(
-                        out=banks[:, s, cols], in0=keys, in1=banks[:, before, cols], op=ADD
-                    )
-                values = multiply_rows([n], range(j, j + TWO), DH)[:, 0 : TWO * DH]
-                nc.scalar.copy(out=v_sb[:, cols], in_=values)
+                xt = xt_banks.tile([P, ROW_WORDS], F32)
+                multiply_rows(xt, [n], range(j, j + TWO), 0)
+                nc.vector.tensor_tensor(
+                    out=banks[:, 1:3, cols],
+                    in0=xt[:, 0 : TWO * DH].unsqueeze(1).to_broadcast([P, 2, TWO * DH]),
+                    in1=banks[:, 0:3:2, cols],
+                    op=ADD,
+                )
+                products = product_banks.tile([P, ROWS * DH], F32)
+                multiply_rows(products, [n], range(j, j + TWO), DH)
+                nc.scalar.copy(out=v_sb[:, cols], in_=products[:, 0 : TWO * DH])
                 nc.sync.dma_start(
                     out=v_chunks[CHUNK_ORDER[n]][:, rows, :], in_=v_rows[:, rows, :]
                 )
@@ -250,7 +258,7 @@ def tile_localxlattention_pa_kernel(tc, kv, Wkv, out_0, out_1):
             if 3 <= n < last:
                 multiply_chunk(n - 2)
         quantise_rows(last, 0, TWO)
-        for j in range(TWO, ROWS):
-            quantise_rows(last, j, 1)
+        quantise_rows(last, TWO, 1)
         multiply_chunk(last - 1)
+        quantise_rows(last, ROWS - 1, 1)
         multiply_last_chunk(last)

from contextlib import ExitStack

import concourse.mybir as mybir
from concourse.masks import make_identity

F32 = mybir.dt.float32
BF16 = mybir.dt.bfloat16
U32 = mybir.dt.uint32
U8 = mybir.dt.uint8
FP8X4 = mybir.dt.float8_e4m3fn_x4
ADD = mybir.AluOpType.add

P = 128
L = 4096
DM = 1024
DH = 128
CHUNK = 512
CHUNKS = L // CHUNK
KV = 2 * DH

FLOPS = 2 * L * DM * KV

PACK = 4
K_PASS = P * PACK
PASSES = DM // K_PASS
PAIRS = 2
ROW_WORDS = DM // 2

ROWS = CHUNK // P
TWO = 2

CHUNK_ORDER = list(range(1, CHUNKS - 1)) + [0, CHUNKS - 1]

MIDDLE = CHUNKS - 2


def tile_localxlattention_pa_kernel(tc, kv, Wkv, out_0, out_1):
    nc = tc.nc

    kv_chunks = kv.rearrange("b (c p j) k -> (b c) p j k", c=CHUNKS, p=P, j=ROWS)
    v_chunks = out_1.rearrange("b (c p j) d -> (b c) p j d", c=CHUNKS, p=P, j=ROWS)
    k_ext_out = out_0.rearrange("b s (p j) d -> b p s j d", p=P, j=ROWS)[0]

    with ExitStack() as ctx:
        ctx.enter_context(tc.manual_schedule())
        consts = ctx.enter_context(tc.tile_pool(name="consts", bufs=1))
        loads = ctx.enter_context(tc.tile_pool(name="loads", bufs=CHUNKS))
        sorts = ctx.enter_context(tc.tile_pool(name="sorts", bufs=2))
        groups = ctx.enter_context(tc.tile_pool(name="groups", bufs=3))
        codes_pool = ctx.enter_context(tc.tile_pool(name="codes_pool", bufs=4))
        results = ctx.enter_context(tc.tile_pool(name="results", bufs=CHUNKS))
        xt_banks = ctx.enter_context(tc.psum_pool(name="xt_banks", bufs=4))
        product_banks = ctx.enter_context(tc.psum_pool(name="product_banks", bufs=4))

        identity = consts.tile([P, P], F32)
        make_identity(nc, identity[:])

        x_tiles = []
        for n in range(CHUNKS):
            x_sb = loads.tile([P, ROWS * DM], BF16)
            x_tiles.append(x_sb)

        def load_rows(n, first, count):
            nc.sync.dma_start(
                out=x_tiles[n][:, first * DM : (first + count) * DM].rearrange(
                    "p (j k) -> p j k", j=count
                ),
                in_=kv_chunks[CHUNK_ORDER[n]][:, first : first + count, :],
            )

        w_raw = consts.tile([P, PASSES * PACK * KV], BF16)
        w_rows = Wkv.rearrange(
            "(g r u w e) n -> g w r u (e n)", g=PASSES, r=P // 2, u=PAIRS, w=2, e=2
        )
        for g in range(PASSES):
            for w in range(2):
                nc.sync.dma_start(
                    out=w_raw[w:P:2, g * PACK * KV : (g + 1) * PACK * KV].rearrange(
                        "r (u c) -> r u c", u=PAIRS
                    ),
                    in_=w_rows[g, w],
                )
        rows_at_once = {0: 1, 1: TWO, 2: TWO, 3: TWO, CHUNKS - 1: TWO}
        for n in range(CHUNKS):
            count = rows_at_once.get(n, ROWS)
            for j in range(0, ROWS, count):
                load_rows(n, j, count)

        w_codes = consts.tile([P, PASSES * KV], U32, align_bytes=64)
        w_scales = consts.tile([P, PASSES * KV], U8, align_bytes=64)

        w_grouped = consts.tile([P, PASSES * KV * PACK], BF16, align_bytes=64)

        def group_weights(g):
            values = slice(g * KV * PACK, (g + 1) * KV * PACK)
            nc.vector.tensor_copy(
                out=w_grouped[:, values].rearrange("p (n t) -> p n t", t=PACK),
                in_=w_raw[:, values].rearrange("p (t n) -> p n t", t=PACK),
            )

        sorted_tiles = {}
        grouped_tiles = {}
        code_tiles = {}

        def sort_rows(n, j, count):
            if j == 0:
                sorted_sb = sorts.tile([P, ROWS * ROW_WORDS], F32)
                sorted_tiles[n] = sorted_sb
            words = slice(j * ROW_WORDS, (j + count) * ROW_WORDS)
            nc.vector.tensor_copy(
                out=sorted_tiles[n][:, words].rearrange(
                    "p (g u c) -> p g u c", g=count * PASSES, u=PAIRS
                ),
                in_=x_tiles[n][:].bitcast(F32)[:, words].rearrange(
                    "p (g r u w) -> p g u r w", g=count * PASSES, u=PAIRS, w=2
                ),
            )

        def transpose_chunk(n):
            grouped = groups.tile([P, ROWS * DM], BF16, align_bytes=64)
            grouped_tiles[n] = grouped
            for j in range(ROWS):
                xt = xt_banks.tile([P, ROW_WORDS], F32)
                for g in range(PASSES):
                    for u in range(PAIRS):
                        s = g * PAIRS + u
                        first = j * ROW_WORDS + s * P
                        nc.tensor.transpose(
                            out=xt[:, s * P : (s + 1) * P],
                            in_=sorted_tiles[n][:, first : first + P],
                            identity=identity[:],
                        )
                on_vector = j == 0 and n == CHUNKS - 1
                copy_out = nc.vector.tensor_copy if on_vector else nc.scalar.copy
                copy_out(
                    out=grouped[:].bitcast(F32)[:, j * ROW_WORDS : (j + 1) * ROW_WORDS].rearrange(
                        "p (g r u) -> p g r u", g=PASSES, u=PAIRS
                    ),
                    in_=xt[:].rearrange("p (g u r) -> p g r u", g=PASSES, u=PAIRS),
                )

        def quantise_rows(n, j, count):
            if j == 0:
                codes = codes_pool.tile([P, ROWS * PASSES * P], U32, align_bytes=64)
                scales = codes_pool.tile([P, ROWS * PASSES * P], U8, align_bytes=64)
                code_tiles[n] = (codes, scales)
            codes, scales = code_tiles[n]
            words = slice(j * PASSES * P, (j + count) * PASSES * P)
            nc.vector.quantize_mx(
                out=codes[:, words].bitcast(FP8X4),
                scales=scales[:, words],
                in_=grouped_tiles[n][:, j * DM : (j + count) * DM],
            )

        def multiply_rows(products, chunks, rows, w_first):
            for i, j in enumerate(rows):
                passes = [(n, g) for n in chunks for g in range(PASSES)]
                for n, g in passes:
                    codes, scales = code_tiles[n]
                    x_cols = slice((j * PASSES + g) * P, (j * PASSES + g + 1) * P)
                    w_cols = slice(g * KV + w_first, g * KV + w_first + DH)
                    nc.tensor.matmul_mx(
                        out=products[:, i * DH : (i + 1) * DH],
                        lhsT=codes[:, x_cols].bitcast(FP8X4),
                        lhsT_scale=scales[:, x_cols],
                        rhs=w_codes[:, w_cols].bitcast(FP8X4),
                        rhs_scale=w_scales[:, w_cols],
                        start=((n, g) == passes[0]),
                        stop=((n, g) == passes[-1]),
                    )

        k_ext_sb = consts.tile([P, 3 * ROWS * DH], F32)
        banks = k_ext_sb[:].rearrange("p (s c) -> p s c", s=3)
        bank_rows = k_ext_sb[:].rearrange("p (s j d) -> p s j d", s=3, j=ROWS)
        all_rows = range(ROWS)

        def multiply_values(n):
            products = product_banks.tile([P, ROWS * DH], F32)
            multiply_rows(products, [n], all_rows, DH)
            v_sb = results.tile([P, ROWS * DH], F32)
            nc.scalar.copy(out=v_sb[:], in_=products[:])
            nc.sync.dma_start(
                out=v_chunks[CHUNK_ORDER[n]], in_=v_sb[:].rearrange("p (j d) -> p j d", j=ROWS)
            )

        def multiply_chunk(n):
            if n == MIDDLE:
                products = product_banks.tile([P, ROWS * DH], F32)
                multiply_rows(products, [n], all_rows, 0)
                nc.vector.tensor_tensor(
                    out=banks[:, 0, :], in0=products[:], in1=banks[:, 2, :], op=ADD
                )
                nc.sync.dma_start(
                    out=k_ext_out[:, 0, :, :], in_=bank_rows[:, 0, :, :]
                )
            elif n % TWO == 1:
                products = product_banks.tile([P, ROWS * DH], F32)
                multiply_rows(products, [n - 1, n], all_rows, 0)
                if n == 1:
                    nc.scalar.copy(out=banks[:, 2, :], in_=products[:])
                else:
                    nc.vector.tensor_tensor(
                        out=banks[:, 2, :], in0=products[:], in1=banks[:, 2, :], op=ADD
                    )
            multiply_values(n)

        def multiply_last_chunk(n):
            v_sb = results.tile([P, ROWS * DH], F32)
            v_rows = v_sb[:].rearrange("p (j d) -> p j d", j=ROWS)
            for j in range(0, ROWS, TWO):
                rows = slice(j, j + TWO)
                cols = slice(j * DH, (j + TWO) * DH)
                xt = xt_banks.tile([P, ROW_WORDS], F32)
                multiply_rows(xt, [n], range(j, j + TWO), 0)
                nc.vector.tensor_tensor(
                    out=banks[:, 1:3, cols],
                    in0=xt[:, 0 : TWO * DH].unsqueeze(1).to_broadcast([P, 2, TWO * DH]),
                    in1=banks[:, 0:3:2, cols],
                    op=ADD,
                )
                products = product_banks.tile([P, ROWS * DH], F32)
                multiply_rows(products, [n], range(j, j + TWO), DH)
                nc.scalar.copy(out=v_sb[:, cols], in_=products[:, 0 : TWO * DH])
                nc.sync.dma_start(
                    out=v_chunks[CHUNK_ORDER[n]][:, rows, :], in_=v_rows[:, rows, :]
                )
                nc.sync.dma_start(
                    out=k_ext_out[:, 1:3, rows, :], in_=bank_rows[:, 1:3, rows, :]
                )

        last = CHUNKS - 1
        group_weights(0)
        sort_rows(0, 0, 1)
        group_weights(1)
        for j in range(1, ROWS):
            sort_rows(0, j, 1)
        nc.vector.quantize_mx(
            out=w_codes[:].bitcast(FP8X4), scales=w_scales[:], in_=w_grouped[:]
        )
        sort_rows(1, 0, TWO)
        for n in range(CHUNKS):
            if n == 1:
                quantise_rows(0, 0, TWO)
                sort_rows(1, TWO, TWO)
                quantise_rows(0, TWO, TWO)
                sort_rows(2, 0, TWO)
                sort_rows(2, TWO, TWO)
            elif n > 1:
                for j in range(0, ROWS, TWO):
                    quantise_rows(n - 1, j, TWO)
                    if n < last:
                        sort_rows(n + 1, j, TWO)
            if n == last:
                multiply_chunk(n - 2)
            transpose_chunk(n)
            if n == 1:
                multiply_chunk(0)
            if 3 <= n < last:
                multiply_chunk(n - 2)
        quantise_rows(last, 0, TWO)
        quantise_rows(last, TWO, 1)
        multiply_chunk(last - 1)
        quantise_rows(last, ROWS - 1, 1)
        multiply_last_chunk(last)
